import numpy as np
import ml_dtypes


def mxq(x, axis, fmt="e4m3"):
    dtype, down = {"e4m3": (ml_dtypes.float8_e4m3fn, 7), "e5m2": (ml_dtypes.float8_e5m2, 14)}[fmt]
    v = np.moveaxis(np.asarray(x, np.float32).astype(ml_dtypes.bfloat16).astype(np.float64), axis, -1)
    blocks = v.reshape(v.shape[:-1] + (-1, 32))
    amax = np.abs(blocks).max(-1, keepdims=True)
    byte = np.maximum(np.where(amax > 0, np.frexp(amax)[1] - 1 + 127, 0) - down, 1)
    scale = np.exp2(byte - 127.0)
    codes = (blocks / scale).astype(np.float32).astype(dtype).astype(np.float64)
    return np.moveaxis((codes * scale).reshape(v.shape), -1, axis)


WIDE = False


def mx_kscale(k):
    if not WIDE:
        return np.ones(k)
    levels = np.array([10, -10, 5, -5, 0])
    a = np.random.permutation(np.resize(levels, k // 512 * 4)).reshape(k // 512, 4)
    idx = np.arange(k)
    return np.exp2(a[idx // 512, idx % 128 // 32])


BF16 = ml_dtypes.bfloat16


def bf(x):
    return np.asarray(x, np.float32).astype(BF16)


def f64(x):
    return np.asarray(x).astype(np.float64)


B, C, K, H, W = 2, 512, 64, 128, 128
N = H * W


def setup_inputs():
    s = mx_kscale(N)
    feats = np.random.standard_normal((B, C, N)) * 4.0 * s.mean() / s
    probs = np.random.standard_normal((B, K, N)) * 2.0 + np.log(s)
    return {"feats": bf(feats.reshape(B, C, H, W)), "probs": bf(probs.reshape(B, K, H, W))}


def reference(feats, probs):
    x = f64(feats).reshape(B, C, N)
    l = f64(probs).reshape(B, K, N)
    e = np.exp(l - l.max(2, keepdims=True))
    ctx = (mxq(e, 2, "e4m3") @ mxq(x, 2, "e4m3").transpose(0, 2, 1)) / e.sum(2, keepdims=True)
    return ctx.transpose(0, 2, 1)[..., None]

@@ -1,0 +1,268 @@
+from contextlib import ExitStack
+
+import concourse.mybir as mybir
+from concourse.masks import make_identity
+
+F32 = mybir.dt.float32
+BF16 = mybir.dt.bfloat16
+U32 = mybir.dt.uint32
+U8 = mybir.dt.uint8
+FP8X4 = mybir.dt.float8_e4m3fn_x4
+ALU = mybir.AluOpType
+ACT = mybir.ActivationFunctionType
+AX = mybir.AxisListType
+
+P = 128
+B, C, K, N = 2, 512, 64, 16384
+FLOPS = 2 * B * K * C * N
+
+PROB_CHUNKS = (4096, 4096, 4096, 2048, 2048)
+NCH = 4096
+TILES = 16
+BANKS = 8
+NBANK = TILES * BANKS
+XB = 5
+LQ = 3
+EPIECE = 1024
+NE = N // EPIECE
+VSET = (3, 7)
+
+
+def tile_spatialgather_module_kernel(tc, feats, probs, out):
+    nc = tc.nc
+    x = feats.rearrange("b c h w -> b c (h w)")
+    l = probs.rearrange("b k h w -> (b k) (h w)")
+    o = out.rearrange("b (t p) k o -> p (b t) (k o)", p=P)
+
+    with ExitStack() as ctx:
+        const = ctx.enter_context(tc.tile_pool(name="const", bufs=1))
+        mxp = ctx.enter_context(tc.tile_pool(name="mxp", bufs=2))
+        xsp = ctx.enter_context(tc.tile_pool(name="xsp", bufs=XB))
+        xgp = ctx.enter_context(tc.tile_pool(name="xgp", bufs=LQ + 3))
+        xcp = ctx.enter_context(tc.tile_pool(name="xcp", bufs=12))
+        enp = ctx.enter_context(tc.tile_pool(name="enp", bufs=4))
+        egp = ctx.enter_context(tc.tile_pool(name="egp", bufs=2))
+        accp = ctx.enter_context(tc.psum_pool(name="accp", bufs=1))
+        tpp = ctx.enter_context(tc.psum_pool(name="tpp", bufs=6))
+        ctx.enter_context(tc.manual_schedule())
+
+        ident_f = const.tile([P, P], F32, name="ident_f")
+        ident_b = const.tile([P, P], BF16, name="ident_b")
+        l_sb = const.tile([P, N], BF16, name="l_sb")
+        e_codes = const.tile([P, N // 4], U32, name="e_codes", align_bytes=64)
+        e_sc = const.tile([P, N // 4], U8, name="e_sc", align_bytes=64)
+        mcol = const.tile([P, 8], F32, name="mcol")
+        mall = const.tile([P, 1], F32, name="mall")
+        negmax = const.tile([P, 1], F32, name="negmax")
+        rs = const.tile([P, NE], F32, name="rs")
+        rtot = const.tile([P, 1], F32, name="rtot")
+        rinv = const.tile([P, 1], F32, name="rinv")
+        scr0 = const.tile([P, 1], F32, name="scr0")
+        scr1 = const.tile([P, 1], F32, name="scr1")
+        ctx_sb = const.tile([P, C], F32, name="ctx_sb")
+        o_sb = const.tile([P, C], F32, name="o_sb")
+        acc = []
+        acc0 = accp.tile([P, C], F32, name="acc0")
+        acc1 = accp.tile([P, C], F32, name="acc1")
+        acc.append(acc0)
+        acc.append(acc1)
+
+        xs_tiles = {}
+        xt_tiles = {}
+        xg_tiles = {}
+        xc_tiles = {}
+        en_tiles = {}
+        et_tiles = {}
+        eg_tiles = {}
+
+        def load_x(tau):
+            j, r = divmod(tau, 4)
+            b, h = divmod(r, 2)
+            xs = xsp.tile([P, 2 * NCH], BF16, name="xs", tag="xs")
+            nc.sync.dma_start(
+                out=xs[:].rearrange("p (a n) -> p a n", a=2),
+                in_=x[b, h * 256 : (h + 1) * 256, j * NCH : (j + 1) * NCH].rearrange("(a p) n -> p a n", p=P),
+            )
+            xs_tiles[tau] = xs
+
+        def x_transposes(s):
+            tau, gl = divmod(s, BANKS)
+            xw = xs_tiles[tau][:].bitcast(F32)
+            xt = tpp.tile([P, 4, P], F32, name="xt", tag="tp")
+            for a in range(2):
+                for u in range(2):
+                    w0 = a * (NCH // 2) + gl * 256 + u * P
+                    nc.tensor.transpose(xt[:, 2 * a + u, :], xw[:, w0 : w0 + P], ident_f[:])
+            xt_tiles[s] = xt
+
+        def x_copy(s):
+            xt = xt_tiles[s]
+            xg = xgp.tile([P, 1024], BF16, name="xg", tag="xg", align_bytes=64)
+            dst = xg[:].bitcast(F32).rearrange("p (a c u) -> p a c u", a=2, u=2)
+            src = xt[:].rearrange("p (a u) c -> p a c u", u=2)
+            if s % BANKS in VSET:
+                nc.vector.tensor_copy(out=dst, in_=src)
+            else:
+                nc.scalar.copy(out=dst, in_=src)
+            xg_tiles[s] = xg
+
+        def x_quant(s):
+            tau, gl = divmod(s, BANKS)
+            gam, h = divmod(tau, 2)
+            xg = xg_tiles[s]
+            if h == 0:
+                xc = xcp.tile([P, C], U32, name="xc", tag="xc", align_bytes=64)
+                xsc = xcp.tile([P, C], U8, name="xsc", tag="xsc", align_bytes=64)
+                xc_tiles[(gam, gl)] = (xc, xsc)
+            xc, xsc = xc_tiles[(gam, gl)]
+            nc.vector.quantize_mx(
+                out=xc[:, h * 256 : (h + 1) * 256].bitcast(FP8X4),
+                scales=xsc[:, h * 256 : (h + 1) * 256],
+                in_=xg[:],
+            )
+
+        def mx_pass(gam, gl):
+            j, b = divmod(gam, 2)
+            g = j * BANKS + gl
+            xc, xsc = xc_tiles[(gam, gl)]
+            nc.tensor.matmul_mx(
+                out=acc[b][:],
+                lhsT=e_codes[:, g * P : (g + 1) * P].bitcast(FP8X4),
+                lhsT_scale=e_sc[:, g * P : (g + 1) * P],
+                rhs=xc[:].bitcast(FP8X4),
+                rhs_scale=xsc[:],
+                start=(g == 0),
+                stop=(g == N // 512 - 1),
+            )
+
+        def e_exp(ei):
+            en = enp.tile([P, EPIECE], BF16, name="en", tag="en")
+            nc.scalar.activation(
+                out=en[:],
+                in_=l_sb[:, ei * EPIECE : (ei + 1) * EPIECE],
+                func=ACT.Exp,
+                bias=negmax[:, 0:1],
+                scale=1.0,
+                accum_out=rs[:, ei : ei + 1],
+            )
+            en_tiles[ei] = en
+
+        def e_transposes(ei):
+            en = en_tiles[ei]
+            v = en[:].rearrange("p (g u q e) -> p g u e q", g=2, u=2, e=2)
+            et = tpp.tile([P, 8, P], BF16, name="et", tag="tp")
+            for g in range(2):
+                for u in range(2):
+                    for e in range(2):
+                        nc.tensor.transpose(et[:, 4 * g + 2 * u + e, :], v[:, g, u, e, :], ident_b[:])
+            et_tiles[ei] = et
+
+        def e_copy(ei):
+            et = et_tiles[ei]
+            eg = egp.tile([P, EPIECE], BF16, name="eg", tag="eg", align_bytes=64)
+            nc.vector.tensor_copy(
+                out=eg[:].rearrange("p (g r t) -> p g r t", g=2, t=4),
+                in_=et[:].rearrange("p (g t) r -> p g r t", t=4),
+            )
+            eg_tiles[ei] = eg
+
+        def e_quant(ei):
+            eg = eg_tiles[ei]
+            w = EPIECE // 4
+            nc.vector.quantize_mx(
+                out=e_codes[:, ei * w : (ei + 1) * w].bitcast(FP8X4),
+                scales=e_sc[:, ei * w : (ei + 1) * w],
+                in_=eg[:],
+            )
+
+        off = 0
+        for w in PROB_CHUNKS:
+            nc.sync.dma_start(out=l_sb[:, off : off + w], in_=l[:, off : off + w])
+            off += w
+        for tau in range(XB):
+            load_x(tau)
+
+        make_identity(nc, ident_f[:])
+        make_identity(nc, ident_b[:])
+        nc.vector.memset(scr0[:], 0.0)
+        nc.scalar.activation(out=scr1[:], in_=scr0[:], func=ACT.Exp)
+
+        off = 0
+        for i, w0 in enumerate(PROB_CHUNKS):
+            src = l_sb[:, off : off + w0]
+            w = w0
+            while w > 256:
+                hw = w // 2
+                m = mxp.tile([P, hw], BF16, name="m%d" % hw, tag="m%d" % hw)
+                nc.vector.tensor_tensor(out=m[:], in0=src[:, 0:hw], in1=src[:, hw:w], op=ALU.max)
+                src = m
+                w = hw
+            nc.vector.tensor_reduce(out=mcol[:, i : i + 1], in_=src[:, 0:w], axis=AX.X, op=ALU.max)
+            off += w0
+        nc.vector.tensor_reduce(out=mall[:], in_=mcol[:, 0 : len(PROB_CHUNKS)], axis=AX.X, op=ALU.max)
+        nc.vector.tensor_scalar(out=negmax[:], in0=mall[:], scalar1=-1.0, scalar2=None, op0=ALU.mult)
+
+        for ei in range(4):
+            e_exp(ei)
+        e_transposes(0)
+        e_copy(0)
+        e_transposes(1)
+        e_copy(1)
+        e_quant(0)
+
+        for s in range(NBANK + LQ):
+            tau, gl = divmod(s, BANKS)
+            ei = tau + 3
+            has_e = 1 <= tau <= NE - 4
+            if s < NBANK:
+                if has_e and gl == 0:
+                    e_exp(ei)
+                x_transposes(s)
+                x_copy(s)
+            if s >= LQ:
+                x_quant(s - LQ)
+            if s == 1:
+                e_transposes(2)
+                e_copy(2)
+                e_quant(1)
+            if s == 3:
+                e_transposes(3)
+                e_copy(3)
+                e_quant(2)
+            if s == 5:
+                e_quant(3)
+            if has_e and gl == 5:
+                e_transposes(ei)
+                e_copy(ei)
+            if has_e and gl == 7:
+                e_quant(ei)
+            if s < NBANK and tau >= 2 and tau % 2 == 0 and gl in (1, 5):
+                gam = tau // 2 - 1
+                for q in range(4):
+                    mx_pass(gam, (gl // 4) * 4 + q)
+            if s < NBANK and gl == 7 and tau + XB < TILES:
+                load_x(tau + XB)
+            if s == (NE - 3) * BANKS:
+                nc.vector.tensor_reduce(out=rtot[:], in_=rs[:], axis=AX.X, op=ALU.add)
+                nc.vector.reciprocal(out=rinv[:], in_=rtot[:])
+            if s == NBANK - 6:
+                nc.scalar.activation(out=ctx_sb[0:64, :], in_=acc[0][0:64, :], func=ACT.Copy, scale=rinv[0:64, 0:1])
+
+        for q in range(BANKS):
+            mx_pass(TILES // 2 - 1, q)
+
+        nc.vector.tensor_scalar(
+            out=ctx_sb[64:128, :], in0=acc[1][64:128, :], scalar1=rinv[64:128, 0:1], scalar2=None, op0=ALU.mult
+        )
+        o_v = o_sb[:].rearrange("p (b t k) -> p b t k", b=B, k=K)
+        for a in range(2):
+            ot = tpp.tile([P, 2, P], F32, name="ot", tag="tp")
+            for i in range(2):
+                t = 2 * a + i
+                nc.tensor.transpose(ot[:, i, :], ctx_sb[:, t * P : (t + 1) * P], ident_f[:])
+            src = ot[:].rearrange("p t (b k) -> p b t k", b=B)
+            if a == 0:
+                nc.vector.tensor_copy(out=o_v[:, :, 0:2, :], in_=src)
+            else:
+                nc.scalar.copy(out=o_v[:, :, 2:4, :], in_=src)
+        nc.sync.dma_start(out=o, in_=o_sb[:].rearrange("p (g k) -> p g k", k=K))

@@ -7,6 +7,7 @@ F32 = mybir.dt.float32
 BF16 = mybir.dt.bfloat16
 U32 = mybir.dt.uint32
 U8 = mybir.dt.uint8
+I32 = mybir.dt.int32
 FP8X4 = mybir.dt.float8_e4m3fn_x4
 ALU = mybir.AluOpType
 ACT = mybir.ActivationFunctionType
@@ -16,16 +17,23 @@ P = 128
 B, C, K, N = 2, 512, 64, 16384
 FLOPS = 2 * B * K * C * N
 
-PROB_CHUNKS = (4096, 4096, 4096, 2048, 2048)
-NCH = 4096
-TILES = 16
-BANKS = 8
-NBANK = TILES * BANKS
-XB = 5
-LQ = 3
-EPIECE = 1024
-NE = N // EPIECE
-VSET = (3, 7)
+PROB_CHUNKS = (2048, 2048, 2048, 2048, 2048, 2048, 2048, 1024, 1024)
+CHUNKS = (1, 1, 2, 4, 4, 4, 4, 4, 4, 2, 1, 1)
+ECH = 2048
+EU = ECH // 512
+NJ = N // ECH
+NU = B * N // 512
+PERIOD = 2 * EU
+ESTEP = 192
+EW = (N // 512) * ESTEP + 64
+XBUFS = {1: 4, 2: 2, 4: 4}
+LQU = 2
+LM = 6
+EPOS = (4, 7, 9, 8, 10, 11)
+EPOS0 = (8, 9, 10, 10, 11, 12)
+MXRUN = 2
+VSTART = (0, 1, 2, 3)
+VP = (9, 11, 13)
 
 
 def tile_spatialgather_module_kernel(tc, feats, probs, out):
@@ -36,36 +44,34 @@ def tile_spatialgather_module_kernel(tc, feats, probs, out):
 
     with ExitStack() as ctx:
         const = ctx.enter_context(tc.tile_pool(name="const", bufs=1))
-        mxp = ctx.enter_context(tc.tile_pool(name="mxp", bufs=2))
-        xsp = ctx.enter_context(tc.tile_pool(name="xsp", bufs=XB))
-        xgp = ctx.enter_context(tc.tile_pool(name="xgp", bufs=LQ + 3))
-        xcp = ctx.enter_context(tc.tile_pool(name="xcp", bufs=12))
-        enp = ctx.enter_context(tc.tile_pool(name="enp", bufs=4))
+        xsp = ctx.enter_context(tc.tile_pool(name="xsp", bufs=1))
+        xgp = ctx.enter_context(tc.tile_pool(name="xgp", bufs=4))
+        xcp = ctx.enter_context(tc.tile_pool(name="xcp", bufs=10))
+        enp = ctx.enter_context(tc.tile_pool(name="enp", bufs=2))
         egp = ctx.enter_context(tc.tile_pool(name="egp", bufs=2))
         accp = ctx.enter_context(tc.psum_pool(name="accp", bufs=1))
-        tpp = ctx.enter_context(tc.psum_pool(name="tpp", bufs=6))
+        tps = ctx.enter_context(tc.psum_pool(name="tps", bufs=4))
+        tpv = ctx.enter_context(tc.psum_pool(name="tpv", bufs=2))
+        tpe = ctx.enter_context(tc.psum_pool(name="tpe", bufs=1))
         ctx.enter_context(tc.manual_schedule())
 
         ident_f = const.tile([P, P], F32, name="ident_f")
         ident_b = const.tile([P, P], BF16, name="ident_b")
         l_sb = const.tile([P, N], BF16, name="l_sb")
-        e_codes = const.tile([P, N // 4], U32, name="e_codes", align_bytes=64)
-        e_sc = const.tile([P, N // 4], U8, name="e_sc", align_bytes=64)
-        mcol = const.tile([P, 8], F32, name="mcol")
+        perm_b = const.tile([P, P], BF16, name="perm_b")
+        e_codes = const.tile([P, EW], U32, name="e_codes", align_bytes=64)
+        e_sc = const.tile([P, EW], U8, name="e_sc", align_bytes=64)
+        mcol = const.tile([P, 16], F32, name="mcol")
         mall = const.tile([P, 1], F32, name="mall")
         negmax = const.tile([P, 1], F32, name="negmax")
-        rs = const.tile([P, NE], F32, name="rs")
+        rs = const.tile([P, NJ], F32, name="rs")
         rtot = const.tile([P, 1], F32, name="rtot")
         rinv = const.tile([P, 1], F32, name="rinv")
         scr0 = const.tile([P, 1], F32, name="scr0")
         scr1 = const.tile([P, 1], F32, name="scr1")
         ctx_sb = const.tile([P, C], F32, name="ctx_sb")
         o_sb = const.tile([P, C], F32, name="o_sb")
-        acc = []
-        acc0 = accp.tile([P, C], F32, name="acc0")
-        acc1 = accp.tile([P, C], F32, name="acc1")
-        acc.append(acc0)
-        acc.append(acc1)
+        acc = accp.tile([P, C], F32, name="acc")
 
         xs_tiles = {}
         xt_tiles = {}
@@ -75,194 +81,224 @@ def tile_spatialgather_module_kernel(tc, feats, probs, out):
         et_tiles = {}
         eg_tiles = {}
 
+        tiles = []
+        units = []
+        g0 = 0
+        for ng in CHUNKS:
+            for b in range(B):
+                for q in range(ng):
+                    units.append((len(tiles), q, b, g0 + q, q == ng - 1))
+                tiles.append((b, g0, ng))
+            g0 += ng
+
         def load_x(tau):
-            j, r = divmod(tau, 4)
-            b, h = divmod(r, 2)
-            xs = xsp.tile([P, 2 * NCH], BF16, name="xs", tag="xs")
+            b, g0, ng = tiles[tau]
+            xs = xsp.tile([P, 4 * 512 * ng], BF16, name="xs%d" % ng, tag="xs%d" % ng, bufs=XBUFS[ng])
             nc.sync.dma_start(
-                out=xs[:].rearrange("p (a n) -> p a n", a=2),
-                in_=x[b, h * 256 : (h + 1) * 256, j * NCH : (j + 1) * NCH].rearrange("(a p) n -> p a n", p=P),
+                out=xs[:].rearrange("p (c n) -> p c n", c=4),
+                in_=x[b, :, g0 * 512 : (g0 + ng) * 512].rearrange("(c p) n -> p c n", p=P),
             )
             xs_tiles[tau] = xs
 
         def x_transposes(s):
-            tau, gl = divmod(s, BANKS)
+            un, a = divmod(s, 2)
+            tau, q = units[un][0], units[un][1]
+            row = 256 * tiles[tau][2]
             xw = xs_tiles[tau][:].bitcast(F32)
-            xt = tpp.tile([P, 4, P], F32, name="xt", tag="tp")
-            for a in range(2):
+            if s % (2 * PERIOD) in VP or s in VSTART:
+                xt = tpv.tile([P, 4, P], F32, name="xtv", tag="xtv")
+            else:
+                xt = tps.tile([P, 4, P], F32, name="xts", tag="xts")
+            for aa in range(2):
                 for u in range(2):
-                    w0 = a * (NCH // 2) + gl * 256 + u * P
-                    nc.tensor.transpose(xt[:, 2 * a + u, :], xw[:, w0 : w0 + P], ident_f[:])
+                    w0 = (2 * a + aa) * row + q * 256 + u * P
+                    nc.tensor.transpose(xt[:, 2 * aa + u, :], xw[:, w0 : w0 + P], ident_f[:])
             xt_tiles[s] = xt
 
         def x_copy(s):
+            un, a = divmod(s, 2)
             xt = xt_tiles[s]
-            xg = xgp.tile([P, 1024], BF16, name="xg", tag="xg", align_bytes=64)
-            dst = xg[:].bitcast(F32).rearrange("p (a c u) -> p a c u", a=2, u=2)
+            if a == 0:
+                xg = xgp.tile([P, 2048], BF16, name="xg", tag="xg", align_bytes=64)
+                xg_tiles[un] = xg
+            xg = xg_tiles[un]
+            dst = xg[:, a * 1024 : (a + 1) * 1024].bitcast(F32).rearrange("p (a c u) -> p a c u", a=2, u=2)
             src = xt[:].rearrange("p (a u) c -> p a c u", u=2)
-            if s % BANKS in VSET:
+            if s % (2 * PERIOD) in VP or s in VSTART:
                 nc.vector.tensor_copy(out=dst, in_=src)
             else:
                 nc.scalar.copy(out=dst, in_=src)
-            xg_tiles[s] = xg
 
-        def x_quant(s):
-            tau, gl = divmod(s, BANKS)
-            gam, h = divmod(tau, 2)
-            xg = xg_tiles[s]
-            if h == 0:
-                xc = xcp.tile([P, C], U32, name="xc", tag="xc", align_bytes=64)
-                xsc = xcp.tile([P, C], U8, name="xsc", tag="xsc", align_bytes=64)
-                xc_tiles[(gam, gl)] = (xc, xsc)
-            xc, xsc = xc_tiles[(gam, gl)]
-            nc.vector.quantize_mx(
-                out=xc[:, h * 256 : (h + 1) * 256].bitcast(FP8X4),
-                scales=xsc[:, h * 256 : (h + 1) * 256],
-                in_=xg[:],
-            )
+        def x_quant(un):
+            xg = xg_tiles[un]
+            xc = xcp.tile([P, C], U32, name="xc", tag="xc", align_bytes=64)
+            xsc = xcp.tile([P, C], U8, name="xsc", tag="xsc", align_bytes=64)
+            xc_tiles[un] = (xc, xsc)
+            nc.vector.quantize_mx(out=xc[:].bitcast(FP8X4), scales=xsc[:], in_=xg[:])
 
-        def mx_pass(gam, gl):
-            j, b = divmod(gam, 2)
-            g = j * BANKS + gl
-            xc, xsc = xc_tiles[(gam, gl)]
+        def mx_pass(un):
+            b, g = units[un][2], units[un][3]
+            xc, xsc = xc_tiles[un]
+            w0 = g * ESTEP + (1 - b) * P
             nc.tensor.matmul_mx(
-                out=acc[b][:],
-                lhsT=e_codes[:, g * P : (g + 1) * P].bitcast(FP8X4),
-                lhsT_scale=e_sc[:, g * P : (g + 1) * P],
+                out=acc[:],
+                lhsT=e_codes[:, w0 : w0 + P].bitcast(FP8X4),
+                lhsT_scale=e_sc[:, w0 : w0 + P],
                 rhs=xc[:].bitcast(FP8X4),
                 rhs_scale=xsc[:],
-                start=(g == 0),
-                stop=(g == N // 512 - 1),
+                start=(un == 0),
+                stop=(un == NU - 1),
             )
 
-        def e_exp(ei):
-            en = enp.tile([P, EPIECE], BF16, name="en", tag="en")
+        def e_exp(jj):
+            en = enp.tile([P, ECH], BF16, name="en", tag="en")
             nc.scalar.activation(
                 out=en[:],
-                in_=l_sb[:, ei * EPIECE : (ei + 1) * EPIECE],
+                in_=l_sb[:, jj * ECH : (jj + 1) * ECH],
                 func=ACT.Exp,
                 bias=negmax[:, 0:1],
                 scale=1.0,
-                accum_out=rs[:, ei : ei + 1],
+                accum_out=rs[:, jj : jj + 1],
             )
-            en_tiles[ei] = en
+            en_tiles[jj] = en
 
         def e_transposes(ei):
-            en = en_tiles[ei]
-            v = en[:].rearrange("p (g u q e) -> p g u e q", g=2, u=2, e=2)
-            et = tpp.tile([P, 8, P], BF16, name="et", tag="tp")
+            jj, hf = divmod(ei, 2)
+            en = en_tiles[jj]
+            v = en[:, hf * 1024 : (hf + 1) * 1024].rearrange("p (g u q e) -> p g u e q", g=2, u=2, e=2)
+            et = tpe.tile([P, 8, P], BF16, name="et", tag="et")
             for g in range(2):
                 for u in range(2):
                     for e in range(2):
-                        nc.tensor.transpose(et[:, 4 * g + 2 * u + e, :], v[:, g, u, e, :], ident_b[:])
+                        nc.tensor.transpose(et[:, 4 * g + 2 * u + e, :], v[:, g, u, e, :], perm_b[:])
             et_tiles[ei] = et
 
         def e_copy(ei):
+            jj, hf = divmod(ei, 2)
             et = et_tiles[ei]
-            eg = egp.tile([P, EPIECE], BF16, name="eg", tag="eg", align_bytes=64)
+            if hf == 0:
+                eg = egp.tile([P, ECH], BF16, name="eg", tag="eg", align_bytes=64)
+                eg_tiles[jj] = eg
+            eg = eg_tiles[jj]
             nc.vector.tensor_copy(
-                out=eg[:].rearrange("p (g r t) -> p g r t", g=2, t=4),
+                out=eg[:, hf * 1024 : (hf + 1) * 1024].rearrange("p (g r t) -> p g r t", g=2, t=4),
                 in_=et[:].rearrange("p (g t) r -> p g r t", t=4),
             )
-            eg_tiles[ei] = eg
 
-        def e_quant(ei):
-            eg = eg_tiles[ei]
-            w = EPIECE // 4
-            nc.vector.quantize_mx(
-                out=e_codes[:, ei * w : (ei + 1) * w].bitcast(FP8X4),
-                scales=e_sc[:, ei * w : (ei + 1) * w],
-                in_=eg[:],
-            )
+        def e_quant(jj):
+            eg = eg_tiles[jj]
+            for q in range(EU):
+                w0 = (jj * EU + q) * ESTEP + 64
+                nc.vector.quantize_mx(
+                    out=e_codes[:, w0 : w0 + P].bitcast(FP8X4),
+                    scales=e_sc[:, w0 : w0 + P],
+                    in_=eg[:, q * 512 : (q + 1) * 512],
+                )
 
         off = 0
         for w in PROB_CHUNKS:
             nc.sync.dma_start(out=l_sb[:, off : off + w], in_=l[:, off : off + w])
             off += w
-        for tau in range(XB):
-            load_x(tau)
+        holder = []
+        for tau in range(len(tiles)):
+            same = [t for t in range(tau) if tiles[t][2] == tiles[tau][2]]
+            nb = XBUFS[tiles[tau][2]]
+            holder.append(same[-nb] if len(same) >= nb else -1)
+        loaded = [0]
+
+        def load_more(done):
+            while loaded[0] < len(tiles) and holder[loaded[0]] <= done:
+                load_x(loaded[0])
+                loaded[0] += 1
+
+        load_more(-1)
 
         make_identity(nc, ident_f[:])
         make_identity(nc, ident_b[:])
+        nc.gpsimd.tensor_copy(out=perm_b[:, 0:64], in_=ident_b[:, 64:128])
+        nc.gpsimd.tensor_copy(out=perm_b[:, 64:128], in_=ident_b[:, 0:64])
         nc.vector.memset(scr0[:], 0.0)
+        for plane, wd in ((e_codes[:].bitcast(I32), ESTEP), (e_sc[:].bitcast(I32), ESTEP // 4)):
+            body = (N // 512) * wd
+            nc.vector.memset(plane[:, 0:body].rearrange("p (g w) -> p g w", w=wd)[:, :, 0 : wd // 3], 0)
+            nc.vector.memset(plane[:, body : body + wd // 3], 0)
         nc.scalar.activation(out=scr1[:], in_=scr0[:], func=ACT.Exp)
 
         off = 0
-        for i, w0 in enumerate(PROB_CHUNKS):
-            src = l_sb[:, off : off + w0]
-            w = w0
-            while w > 256:
-                hw = w // 2
-                m = mxp.tile([P, hw], BF16, name="m%d" % hw, tag="m%d" % hw)
-                nc.vector.tensor_tensor(out=m[:], in0=src[:, 0:hw], in1=src[:, hw:w], op=ALU.max)
-                src = m
-                w = hw
-            nc.vector.tensor_reduce(out=mcol[:, i : i + 1], in_=src[:, 0:w], axis=AX.X, op=ALU.max)
-            off += w0
+        for i, w in enumerate(PROB_CHUNKS):
+            junk = enp.tile([P, w], BF16, name="junk", tag="en")
+            nc.vector.tensor_scalar(
+                out=junk[:],
+                in0=l_sb[:, off : off + w],
+                scalar1=0.0,
+                scalar2=None,
+                op0=ALU.add,
+                op1=ALU.max,
+                accum_out=mcol[:, i : i + 1],
+            )
+            off += w
         nc.vector.tensor_reduce(out=mall[:], in_=mcol[:, 0 : len(PROB_CHUNKS)], axis=AX.X, op=ALU.max)
         nc.vector.tensor_scalar(out=negmax[:], in0=mall[:], scalar1=-1.0, scalar2=None, op0=ALU.mult)
 
-        for ei in range(4):
-            e_exp(ei)
-        e_transposes(0)
-        e_copy(0)
-        e_transposes(1)
-        e_copy(1)
-        e_quant(0)
+        before = {}
+        after = {}
 
-        for s in range(NBANK + LQ):
-            tau, gl = divmod(s, BANKS)
-            ei = tau + 3
-            has_e = 1 <= tau <= NE - 4
-            if s < NBANK:
-                if has_e and gl == 0:
-                    e_exp(ei)
-                x_transposes(s)
-                x_copy(s)
-            if s >= LQ:
-                x_quant(s - LQ)
-            if s == 1:
-                e_transposes(2)
-                e_copy(2)
-                e_quant(1)
-            if s == 3:
-                e_transposes(3)
-                e_copy(3)
-                e_quant(2)
-            if s == 5:
-                e_quant(3)
-            if has_e and gl == 5:
-                e_transposes(ei)
-                e_copy(ei)
-            if has_e and gl == 7:
-                e_quant(ei)
-            if s < NBANK and tau >= 2 and tau % 2 == 0 and gl in (1, 5):
-                gam = tau // 2 - 1
-                for q in range(4):
-                    mx_pass(gam, (gl // 4) * 4 + q)
-            if s < NBANK and gl == 7 and tau + XB < TILES:
-                load_x(tau + XB)
-            if s == (NE - 3) * BANKS:
+        def at(table, un, fn, arg):
+            table[un] = table.get(un, []) + [(fn, arg)]
+
+        for jj in range(NJ):
+            base = (jj - 1) * PERIOD
+            pos = EPOS if jj > 0 else EPOS0
+            if jj > 0:
+                at(before, base + pos[0], e_exp, jj)
+            for hf in range(2):
+                at(after, base + pos[1 + hf], e_transposes, 2 * jj + hf)
+                at(after, base + pos[3 + hf], e_copy, 2 * jj + hf)
+            at(after, base + pos[5], e_quant, jj)
+
+        e_exp(0)
+        for un in range(NU + LM):
+            live = un < NU
+            for fn, arg in before.get(un, []):
+                fn(arg)
+            if live:
+                x_transposes(2 * un)
+                x_transposes(2 * un + 1)
+                x_copy(2 * un)
+                x_copy(2 * un + 1)
+            if LQU <= un < NU + LQU:
+                x_quant(un - LQU)
+            for fn, arg in after.get(un, []):
+                fn(arg)
+            last = un - LM
+            if last >= 0 and last % MXRUN == MXRUN - 1:
+                for k in range(MXRUN):
+                    mx_pass(last - MXRUN + 1 + k)
+            if live and units[un][4]:
+                load_more(units[un][0])
+            if un == NU - PERIOD + 1:
                 nc.vector.tensor_reduce(out=rtot[:], in_=rs[:], axis=AX.X, op=ALU.add)
                 nc.vector.reciprocal(out=rinv[:], in_=rtot[:])
-            if s == NBANK - 6:
-                nc.scalar.activation(out=ctx_sb[0:64, :], in_=acc[0][0:64, :], func=ACT.Copy, scale=rinv[0:64, 0:1])
 
-        for q in range(BANKS):
-            mx_pass(TILES // 2 - 1, q)
-
-        nc.vector.tensor_scalar(
-            out=ctx_sb[64:128, :], in0=acc[1][64:128, :], scalar1=rinv[64:128, 0:1], scalar2=None, op0=ALU.mult
-        )
         o_v = o_sb[:].rearrange("p (b t k) -> p b t k", b=B, k=K)
         for a in range(2):
-            ot = tpp.tile([P, 2, P], F32, name="ot", tag="tp")
+            nc.vector.tensor_scalar(
+                out=ctx_sb[:, a * 256 : (a + 1) * 256],
+                in0=acc[:, a * 256 : (a + 1) * 256],
+                scalar1=rinv[:, 0:1],
+                scalar2=None,
+                op0=ALU.mult,
+            )
+            if a == 0:
+                ot = tpv.tile([P, 2, P], F32, name="otv", tag="xtv")
+            else:
+                ot = tps.tile([P, 2, P], F32, name="ots", tag="xts")
             for i in range(2):
                 t = 2 * a + i
                 nc.tensor.transpose(ot[:, i, :], ctx_sb[:, t * P : (t + 1) * P], ident_f[:])
             src = ot[:].rearrange("p t (b k) -> p b t k", b=B)
             if a == 0:
-                nc.vector.tensor_copy(out=o_v[:, :, 0:2, :], in_=src)
+                nc.scalar.copy(out=o_v[:, :, 0:2, :], in_=src)
             else:
-                nc.scalar.copy(out=o_v[:, :, 2:4, :], in_=src)
+                nc.vector.tensor_copy(out=o_v[:, :, 2:4, :], in_=src)
         nc.sync.dma_start(out=o, in_=o_sb[:].rearrange("p (g k) -> p g k", k=K))

@@ -25,13 +25,14 @@ NJ = N // ECH
 NU = B * N // 512
 PERIOD = 2 * EU
 ESTEP = 192
-EW = (N // 512) * ESTEP + 64
+ER = 12
+EW = ER * ESTEP + 64
 XBUFS = {1: 4, 2: 2, 4: 4}
 LQU = 2
-LM = 6
+LM = 8
 EPOS = (4, 7, 9, 8, 10, 11)
 EPOS0 = (8, 9, 10, 10, 11, 12)
-MXRUN = 2
+MXRUN = 4
 VSTART = (0, 1, 2, 3)
 VP = (9, 11, 13)
 
@@ -46,7 +47,7 @@ def tile_spatialgather_module_kernel(tc, feats, probs, out):
         const = ctx.enter_context(tc.tile_pool(name="const", bufs=1))
         xsp = ctx.enter_context(tc.tile_pool(name="xsp", bufs=1))
         xgp = ctx.enter_context(tc.tile_pool(name="xgp", bufs=4))
-        xcp = ctx.enter_context(tc.tile_pool(name="xcp", bufs=10))
+        xcp = ctx.enter_context(tc.tile_pool(name="xcp", bufs=12))
         enp = ctx.enter_context(tc.tile_pool(name="enp", bufs=2))
         egp = ctx.enter_context(tc.tile_pool(name="egp", bufs=2))
         accp = ctx.enter_context(tc.psum_pool(name="accp", bufs=1))
@@ -139,7 +140,7 @@ def tile_spatialgather_module_kernel(tc, feats, probs, out):
         def mx_pass(un):
             b, g = units[un][2], units[un][3]
             xc, xsc = xc_tiles[un]
-            w0 = g * ESTEP + (1 - b) * P
+            w0 = (g % ER) * ESTEP + (1 - b) * P
             nc.tensor.matmul_mx(
                 out=acc[:],
                 lhsT=e_codes[:, w0 : w0 + P].bitcast(FP8X4),
@@ -153,8 +154,8 @@ def tile_spatialgather_module_kernel(tc, feats, probs, out):
         def e_exp(jj):
             en = enp.tile([P, ECH], BF16, name="en", tag="en")
             nc.scalar.activation(
-                out=en[:],
-                in_=l_sb[:, jj * ECH : (jj + 1) * ECH],
+                out=en[:].rearrange("p (s e q) -> p s e q", e=2, q=P),
+                in_=l_sb[:, jj * ECH : (jj + 1) * ECH].rearrange("p (s q e) -> p s e q", e=2, q=P),
                 func=ACT.Exp,
                 bias=negmax[:, 0:1],
                 scale=1.0,
@@ -165,7 +166,7 @@ def tile_spatialgather_module_kernel(tc, feats, probs, out):
         def e_transposes(ei):
             jj, hf = divmod(ei, 2)
             en = en_tiles[jj]
-            v = en[:, hf * 1024 : (hf + 1) * 1024].rearrange("p (g u q e) -> p g u e q", g=2, u=2, e=2)
+            v = en[:, hf * 1024 : (hf + 1) * 1024].rearrange("p (g u e q) -> p g u e q", g=2, u=2, e=2)
             et = tpe.tile([P, 8, P], BF16, name="et", tag="et")
             for g in range(2):
                 for u in range(2):
@@ -188,7 +189,7 @@ def tile_spatialgather_module_kernel(tc, feats, probs, out):
         def e_quant(jj):
             eg = eg_tiles[jj]
             for q in range(EU):
-                w0 = (jj * EU + q) * ESTEP + 64
+                w0 = ((jj * EU + q) % ER) * ESTEP + 64
                 nc.vector.quantize_mx(
                     out=e_codes[:, w0 : w0 + P].bitcast(FP8X4),
                     scales=e_sc[:, w0 : w0 + P],
@@ -219,7 +220,7 @@ def tile_spatialgather_module_kernel(tc, feats, probs, out):
         nc.gpsimd.tensor_copy(out=perm_b[:, 64:128], in_=ident_b[:, 0:64])
         nc.vector.memset(scr0[:], 0.0)
         for plane, wd in ((e_codes[:].bitcast(I32), ESTEP), (e_sc[:].bitcast(I32), ESTEP // 4)):
-            body = (N // 512) * wd
+            body = ER * wd
             nc.vector.memset(plane[:, 0:body].rearrange("p (g w) -> p g w", w=wd)[:, :, 0 : wd // 3], 0)
             nc.vector.memset(plane[:, body : body + wd // 3], 0)
         nc.scalar.activation(out=scr1[:], in_=scr0[:], func=ACT.Exp)

@@ -34,7 +34,7 @@ EPOS = (4, 7, 9, 8, 10, 11)
 EPOS0 = (8, 9, 10, 10, 11, 12)
 MXRUN = 4
 VSTART = (0, 1, 2, 3)
-VP = (9, 11, 13)
+VP = (9, 11, 13, 2)
 
 
 def tile_spatialgather_module_kernel(tc, feats, probs, out):
@@ -154,8 +154,8 @@ def tile_spatialgather_module_kernel(tc, feats, probs, out):
         def e_exp(jj):
             en = enp.tile([P, ECH], BF16, name="en", tag="en")
             nc.scalar.activation(
-                out=en[:].rearrange("p (s e q) -> p s e q", e=2, q=P),
-                in_=l_sb[:, jj * ECH : (jj + 1) * ECH].rearrange("p (s q e) -> p s e q", e=2, q=P),
+                out=en[:],
+                in_=l_sb[:, jj * ECH : (jj + 1) * ECH],
                 func=ACT.Exp,
                 bias=negmax[:, 0:1],
                 scale=1.0,
@@ -166,7 +166,7 @@ def tile_spatialgather_module_kernel(tc, feats, probs, out):
         def e_transposes(ei):
             jj, hf = divmod(ei, 2)
             en = en_tiles[jj]
-            v = en[:, hf * 1024 : (hf + 1) * 1024].rearrange("p (g u e q) -> p g u e q", g=2, u=2, e=2)
+            v = en[:, hf * 1024 : (hf + 1) * 1024].rearrange("p (g u q e) -> p g u e q", g=2, u=2, e=2)
             et = tpe.tile([P, 8, P], BF16, name="et", tag="et")
             for g in range(2):
                 for u in range(2):

@@ -25,14 +25,13 @@ NJ = N // ECH
 NU = B * N // 512
 PERIOD = 2 * EU
 ESTEP = 192
-ER = 12
-EW = ER * ESTEP + 64
+EW = (N // 512) * ESTEP + 64
 XBUFS = {1: 4, 2: 2, 4: 4}
 LQU = 2
-LM = 8
+LM = 6
 EPOS = (4, 7, 9, 8, 10, 11)
 EPOS0 = (8, 9, 10, 10, 11, 12)
-MXRUN = 4
+MXRUN = 2
 VSTART = (0, 1, 2, 3)
 VP = (9, 11, 13, 2)
 
@@ -47,7 +46,7 @@ def tile_spatialgather_module_kernel(tc, feats, probs, out):
         const = ctx.enter_context(tc.tile_pool(name="const", bufs=1))
         xsp = ctx.enter_context(tc.tile_pool(name="xsp", bufs=1))
         xgp = ctx.enter_context(tc.tile_pool(name="xgp", bufs=4))
-        xcp = ctx.enter_context(tc.tile_pool(name="xcp", bufs=12))
+        xcp = ctx.enter_context(tc.tile_pool(name="xcp", bufs=10))
         enp = ctx.enter_context(tc.tile_pool(name="enp", bufs=2))
         egp = ctx.enter_context(tc.tile_pool(name="egp", bufs=2))
         accp = ctx.enter_context(tc.psum_pool(name="accp", bufs=1))
@@ -140,7 +139,7 @@ def tile_spatialgather_module_kernel(tc, feats, probs, out):
         def mx_pass(un):
             b, g = units[un][2], units[un][3]
             xc, xsc = xc_tiles[un]
-            w0 = (g % ER) * ESTEP + (1 - b) * P
+            w0 = g * ESTEP + (1 - b) * P
             nc.tensor.matmul_mx(
                 out=acc[:],
                 lhsT=e_codes[:, w0 : w0 + P].bitcast(FP8X4),
@@ -189,7 +188,7 @@ def tile_spatialgather_module_kernel(tc, feats, probs, out):
         def e_quant(jj):
             eg = eg_tiles[jj]
             for q in range(EU):
-                w0 = ((jj * EU + q) % ER) * ESTEP + 64
+                w0 = (jj * EU + q) * ESTEP + 64
                 nc.vector.quantize_mx(
                     out=e_codes[:, w0 : w0 + P].bitcast(FP8X4),
                     scales=e_sc[:, w0 : w0 + P],
@@ -220,7 +219,7 @@ def tile_spatialgather_module_kernel(tc, feats, probs, out):
         nc.gpsimd.tensor_copy(out=perm_b[:, 64:128], in_=ident_b[:, 0:64])
         nc.vector.memset(scr0[:], 0.0)
         for plane, wd in ((e_codes[:].bitcast(I32), ESTEP), (e_sc[:].bitcast(I32), ESTEP // 4)):
-            body = ER * wd
+            body = (N // 512) * wd
             nc.vector.memset(plane[:, 0:body].rearrange("p (g w) -> p g w", w=wd)[:, :, 0 : wd // 3], 0)
             nc.vector.memset(plane[:, body : body + wd // 3], 0)
         nc.scalar.activation(out=scr1[:], in_=scr0[:], func=ACT.Exp)

@@ -17,23 +17,23 @@ P = 128
 B, C, K, N = 2, 512, 64, 16384
 FLOPS = 2 * B * K * C * N
 
+NP = N // 512
 PROB_CHUNKS = (2048, 2048, 2048, 2048, 2048, 2048, 2048, 1024, 1024)
 CHUNKS = (1, 1, 2, 4, 4, 4, 4, 4, 4, 2, 1, 1)
-ECH = 2048
-EU = ECH // 512
-NJ = N // ECH
-NU = B * N // 512
-PERIOD = 2 * EU
+XBUFS = {1: 4, 2: 2, 4: 5}
 ESTEP = 192
-EW = (N // 512) * ESTEP + 64
-XBUFS = {1: 4, 2: 2, 4: 4}
-LQU = 2
-LM = 6
-EPOS = (4, 7, 9, 8, 10, 11)
-EPOS0 = (8, 9, 10, 10, 11, 12)
-MXRUN = 2
-VSTART = (0, 1, 2, 3)
-VP = (9, 11, 13, 2)
+ER = 8
+EXP_OFF = -2
+ET_OFF = -1
+EC_OFF = 0
+EQ_OFF = 0
+Q_OFF = 1
+MX_OFF = 3
+XGB = 3
+XCB = 4
+EARLY = 3
+WARM = ((3, 4), (4, 4), (5, 4))
+VSKIP = 0
 
 
 def tile_spatialgather_module_kernel(tc, feats, probs, out):
@@ -45,10 +45,11 @@ def tile_spatialgather_module_kernel(tc, feats, probs, out):
     with ExitStack() as ctx:
         const = ctx.enter_context(tc.tile_pool(name="const", bufs=1))
         xsp = ctx.enter_context(tc.tile_pool(name="xsp", bufs=1))
-        xgp = ctx.enter_context(tc.tile_pool(name="xgp", bufs=4))
-        xcp = ctx.enter_context(tc.tile_pool(name="xcp", bufs=10))
-        enp = ctx.enter_context(tc.tile_pool(name="enp", bufs=2))
-        egp = ctx.enter_context(tc.tile_pool(name="egp", bufs=2))
+        xgp = ctx.enter_context(tc.tile_pool(name="xgp", bufs=XGB))
+        xcp = ctx.enter_context(tc.tile_pool(name="xcp", bufs=XCB))
+        jkp = ctx.enter_context(tc.tile_pool(name="jkp", bufs=2))
+        enp = ctx.enter_context(tc.tile_pool(name="enp", bufs=4))
+        egp = ctx.enter_context(tc.tile_pool(name="egp", bufs=3))
         accp = ctx.enter_context(tc.psum_pool(name="accp", bufs=1))
         tps = ctx.enter_context(tc.psum_pool(name="tps", bufs=4))
         tpv = ctx.enter_context(tc.psum_pool(name="tpv", bufs=2))
@@ -57,14 +58,14 @@ def tile_spatialgather_module_kernel(tc, feats, probs, out):
 
         ident_f = const.tile([P, P], F32, name="ident_f")
         ident_b = const.tile([P, P], BF16, name="ident_b")
-        l_sb = const.tile([P, N], BF16, name="l_sb")
         perm_b = const.tile([P, P], BF16, name="perm_b")
-        e_codes = const.tile([P, EW], U32, name="e_codes", align_bytes=64)
-        e_sc = const.tile([P, EW], U8, name="e_sc", align_bytes=64)
+        l_sb = const.tile([P, N], BF16, name="l_sb")
+        e_codes = const.tile([P, ER * ESTEP + 64], U32, name="e_codes", align_bytes=64)
+        e_sc = const.tile([P, ER * ESTEP + 64], U8, name="e_sc", align_bytes=64)
         mcol = const.tile([P, 16], F32, name="mcol")
         mall = const.tile([P, 1], F32, name="mall")
         negmax = const.tile([P, 1], F32, name="negmax")
-        rs = const.tile([P, NJ], F32, name="rs")
+        rs = const.tile([P, NP], F32, name="rs")
         rtot = const.tile([P, 1], F32, name="rtot")
         rinv = const.tile([P, 1], F32, name="rinv")
         scr0 = const.tile([P, 1], F32, name="scr0")
@@ -72,6 +73,11 @@ def tile_spatialgather_module_kernel(tc, feats, probs, out):
         ctx_sb = const.tile([P, C], F32, name="ctx_sb")
         o_sb = const.tile([P, C], F32, name="o_sb")
         acc = accp.tile([P, C], F32, name="acc")
+        zc = const.tile([P, C], U32, name="zc", align_bytes=64)
+        zs = const.tile([P, C], U8, name="zs", align_bytes=64)
+        zb = const.tile([P, 4 * C], BF16, name="zb", align_bytes=64)
+        gate_c = const.tile([P, len(WARM) * P], U32, name="gate_c", align_bytes=64)
+        gate_s = const.tile([P, len(WARM) * P], U8, name="gate_s", align_bytes=64)
 
         xs_tiles = {}
         xt_tiles = {}
@@ -87,7 +93,7 @@ def tile_spatialgather_module_kernel(tc, feats, probs, out):
         for ng in CHUNKS:
             for b in range(B):
                 for q in range(ng):
-                    units.append((len(tiles), q, b, g0 + q, q == ng - 1))
+                    units.append((len(tiles), q, b, g0 + q))
                 tiles.append((b, g0, ng))
             g0 += ng
 
@@ -100,12 +106,14 @@ def tile_spatialgather_module_kernel(tc, feats, probs, out):
             )
             xs_tiles[tau] = xs
 
-        def x_transposes(s):
-            un, a = divmod(s, 2)
-            tau, q = units[un][0], units[un][1]
+        def on_vector(st, i, a):
+            return i == 1 and a == 1 and not (VSKIP and st % VSKIP == VSKIP - 1)
+
+        def x_transposes(st, i, a):
+            tau, q = units[2 * st + i][0], units[2 * st + i][1]
             row = 256 * tiles[tau][2]
             xw = xs_tiles[tau][:].bitcast(F32)
-            if s % (2 * PERIOD) in VP or s in VSTART:
+            if on_vector(st, i, a):
                 xt = tpv.tile([P, 4, P], F32, name="xtv", tag="xtv")
             else:
                 xt = tps.tile([P, 4, P], F32, name="xts", tag="xts")
@@ -113,87 +121,85 @@ def tile_spatialgather_module_kernel(tc, feats, probs, out):
                 for u in range(2):
                     w0 = (2 * a + aa) * row + q * 256 + u * P
                     nc.tensor.transpose(xt[:, 2 * aa + u, :], xw[:, w0 : w0 + P], ident_f[:])
-            xt_tiles[s] = xt
+            xt_tiles[(st, i, a)] = xt
 
-        def x_copy(s):
-            un, a = divmod(s, 2)
-            xt = xt_tiles[s]
-            if a == 0:
-                xg = xgp.tile([P, 2048], BF16, name="xg", tag="xg", align_bytes=64)
-                xg_tiles[un] = xg
-            xg = xg_tiles[un]
-            dst = xg[:, a * 1024 : (a + 1) * 1024].bitcast(F32).rearrange("p (a c u) -> p a c u", a=2, u=2)
+        def x_copy(st, i, a):
+            xt = xt_tiles[(st, i, a)]
+            if i == 0 and a == 0:
+                xg = xgp.tile([P, 4096], BF16, name="xg", tag="xg", align_bytes=64)
+                xg_tiles[st] = xg
+            xg = xg_tiles[st]
+            h0 = (2 * i + a) * 1024
+            dst = xg[:, h0 : h0 + 1024].bitcast(F32).rearrange("p (a c u) -> p a c u", a=2, u=2)
             src = xt[:].rearrange("p (a u) c -> p a c u", u=2)
-            if s % (2 * PERIOD) in VP or s in VSTART:
+            if on_vector(st, i, a):
                 nc.vector.tensor_copy(out=dst, in_=src)
             else:
                 nc.scalar.copy(out=dst, in_=src)
 
-        def x_quant(un):
-            xg = xg_tiles[un]
-            xc = xcp.tile([P, C], U32, name="xc", tag="xc", align_bytes=64)
-            xsc = xcp.tile([P, C], U8, name="xsc", tag="xsc", align_bytes=64)
-            xc_tiles[un] = (xc, xsc)
-            nc.vector.quantize_mx(out=xc[:].bitcast(FP8X4), scales=xsc[:], in_=xg[:])
+        def x_quant(st):
+            xc = xcp.tile([P, 2 * C], U32, name="xc", tag="xc", align_bytes=64)
+            xsc = xcp.tile([P, 2 * C], U8, name="xsc", tag="xsc", align_bytes=64)
+            xc_tiles[st] = (xc, xsc)
+            nc.vector.quantize_mx(out=xc[:].bitcast(FP8X4), scales=xsc[:], in_=xg_tiles[st][:])
 
-        def mx_pass(un):
-            b, g = units[un][2], units[un][3]
-            xc, xsc = xc_tiles[un]
-            w0 = g * ESTEP + (1 - b) * P
+        def mx_pass(st, i):
+            b, g = units[2 * st + i][2], units[2 * st + i][3]
+            xc, xsc = xc_tiles[st]
+            w0 = (g % ER) * ESTEP + (1 - b) * P
             nc.tensor.matmul_mx(
                 out=acc[:],
                 lhsT=e_codes[:, w0 : w0 + P].bitcast(FP8X4),
                 lhsT_scale=e_sc[:, w0 : w0 + P],
-                rhs=xc[:].bitcast(FP8X4),
-                rhs_scale=xsc[:],
-                start=(un == 0),
-                stop=(un == NU - 1),
+                rhs=xc[:, i * C : (i + 1) * C].bitcast(FP8X4),
+                rhs_scale=xsc[:, i * C : (i + 1) * C],
+                start=False,
+                stop=(st == NP - 1 and i == 1),
             )
 
-        def e_exp(jj):
-            en = enp.tile([P, ECH], BF16, name="en", tag="en")
+        def idle_pass(codes, scale, first):
+            nc.tensor.matmul_mx(
+                out=acc[:],
+                lhsT=codes.bitcast(FP8X4),
+                lhsT_scale=scale,
+                rhs=zc[:].bitcast(FP8X4),
+                rhs_scale=zs[:],
+                start=first,
+                stop=False,
+            )
+
+        def e_exp(g):
+            en = enp.tile([P, 512], BF16, name="en", tag="en")
             nc.scalar.activation(
                 out=en[:],
-                in_=l_sb[:, jj * ECH : (jj + 1) * ECH],
+                in_=l_sb[:, g * 512 : (g + 1) * 512],
                 func=ACT.Exp,
                 bias=negmax[:, 0:1],
                 scale=1.0,
-                accum_out=rs[:, jj : jj + 1],
+                accum_out=rs[:, g : g + 1],
             )
-            en_tiles[jj] = en
+            en_tiles[g] = en
 
-        def e_transposes(ei):
-            jj, hf = divmod(ei, 2)
-            en = en_tiles[jj]
-            v = en[:, hf * 1024 : (hf + 1) * 1024].rearrange("p (g u q e) -> p g u e q", g=2, u=2, e=2)
-            et = tpe.tile([P, 8, P], BF16, name="et", tag="et")
-            for g in range(2):
-                for u in range(2):
-                    for e in range(2):
-                        nc.tensor.transpose(et[:, 4 * g + 2 * u + e, :], v[:, g, u, e, :], perm_b[:])
-            et_tiles[ei] = et
+        def e_transposes(g):
+            v = en_tiles[g][:].rearrange("p (u q e) -> p u e q", u=2, e=2)
+            et = tpe.tile([P, 4, P], BF16, name="et", tag="et")
+            for u in range(2):
+                for e in range(2):
+                    nc.tensor.transpose(et[:, 2 * u + e, :], v[:, u, e, :], perm_b[:])
+            et_tiles[g] = et
 
-        def e_copy(ei):
-            jj, hf = divmod(ei, 2)
-            et = et_tiles[ei]
-            if hf == 0:
-                eg = egp.tile([P, ECH], BF16, name="eg", tag="eg", align_bytes=64)
-                eg_tiles[jj] = eg
-            eg = eg_tiles[jj]
+        def e_copy(g):
+            eg = egp.tile([P, 512], BF16, name="eg", tag="eg", align_bytes=64)
             nc.vector.tensor_copy(
-                out=eg[:, hf * 1024 : (hf + 1) * 1024].rearrange("p (g r t) -> p g r t", g=2, t=4),
-                in_=et[:].rearrange("p (g t) r -> p g r t", t=4),
+                out=eg[:].rearrange("p (r t) -> p r t", t=4), in_=et_tiles[g][:].rearrange("p t r -> p r t")
             )
+            eg_tiles[g] = eg
 
-        def e_quant(jj):
-            eg = eg_tiles[jj]
-            for q in range(EU):
-                w0 = (jj * EU + q) * ESTEP + 64
-                nc.vector.quantize_mx(
-                    out=e_codes[:, w0 : w0 + P].bitcast(FP8X4),
-                    scales=e_sc[:, w0 : w0 + P],
-                    in_=eg[:, q * 512 : (q + 1) * 512],
-                )
+        def e_quant(g):
+            w0 = (g % ER) * ESTEP + 64
+            nc.vector.quantize_mx(
+                out=e_codes[:, w0 : w0 + P].bitcast(FP8X4), scales=e_sc[:, w0 : w0 + P], in_=eg_tiles[g][:]
+            )
 
         off = 0
         for w in PROB_CHUNKS:
@@ -218,15 +224,15 @@ def tile_spatialgather_module_kernel(tc, feats, probs, out):
         nc.gpsimd.tensor_copy(out=perm_b[:, 0:64], in_=ident_b[:, 64:128])
         nc.gpsimd.tensor_copy(out=perm_b[:, 64:128], in_=ident_b[:, 0:64])
         nc.vector.memset(scr0[:], 0.0)
-        for plane, wd in ((e_codes[:].bitcast(I32), ESTEP), (e_sc[:].bitcast(I32), ESTEP // 4)):
-            body = (N // 512) * wd
-            nc.vector.memset(plane[:, 0:body].rearrange("p (g w) -> p g w", w=wd)[:, :, 0 : wd // 3], 0)
-            nc.vector.memset(plane[:, body : body + wd // 3], 0)
+        nc.vector.memset(e_codes[:].bitcast(I32), 0)
+        nc.vector.memset(e_sc[:].bitcast(I32), 0)
+        nc.vector.memset(zb[:].bitcast(I32), 0)
+        nc.vector.quantize_mx(out=zc[:].bitcast(FP8X4), scales=zs[:], in_=zb[:])
         nc.scalar.activation(out=scr1[:], in_=scr0[:], func=ACT.Exp)
 
         off = 0
         for i, w in enumerate(PROB_CHUNKS):
-            junk = enp.tile([P, w], BF16, name="junk", tag="en")
+            junk = jkp.tile([P, w], BF16, name="junk", tag="junk")
             nc.vector.tensor_scalar(
                 out=junk[:],
                 in0=l_sb[:, off : off + w],
@@ -237,46 +243,52 @@ def tile_spatialgather_module_kernel(tc, feats, probs, out):
                 accum_out=mcol[:, i : i + 1],
             )
             off += w
+            for k, (chunk, count) in enumerate(WARM):
+                if chunk == i:
+                    cols = slice(k * P, (k + 1) * P)
+                    nc.vector.quantize_mx(out=gate_c[:, cols].bitcast(FP8X4), scales=gate_s[:, cols], in_=zb[:, 0:C])
+                    for j in range(count):
+                        idle_pass(gate_c[:, cols], gate_s[:, cols], k == 0 and j == 0)
         nc.vector.tensor_reduce(out=mall[:], in_=mcol[:, 0 : len(PROB_CHUNKS)], axis=AX.X, op=ALU.max)
         nc.vector.tensor_scalar(out=negmax[:], in0=mall[:], scalar1=-1.0, scalar2=None, op0=ALU.mult)
 
-        before = {}
-        after = {}
+        def e_work(st, off, fn):
+            if 0 <= st - off < NP:
+                fn(st - off)
 
-        def at(table, un, fn, arg):
-            table[un] = table.get(un, []) + [(fn, arg)]
-
-        for jj in range(NJ):
-            base = (jj - 1) * PERIOD
-            pos = EPOS if jj > 0 else EPOS0
-            if jj > 0:
-                at(before, base + pos[0], e_exp, jj)
-            for hf in range(2):
-                at(after, base + pos[1 + hf], e_transposes, 2 * jj + hf)
-                at(after, base + pos[3 + hf], e_copy, 2 * jj + hf)
-            at(after, base + pos[5], e_quant, jj)
-
-        e_exp(0)
-        for un in range(NU + LM):
-            live = un < NU
-            for fn, arg in before.get(un, []):
-                fn(arg)
-            if live:
-                x_transposes(2 * un)
-                x_transposes(2 * un + 1)
-                x_copy(2 * un)
-                x_copy(2 * un + 1)
-            if LQU <= un < NU + LQU:
-                x_quant(un - LQU)
-            for fn, arg in after.get(un, []):
-                fn(arg)
-            last = un - LM
-            if last >= 0 and last % MXRUN == MXRUN - 1:
-                for k in range(MXRUN):
-                    mx_pass(last - MXRUN + 1 + k)
-            if live and units[un][4]:
-                load_more(units[un][0])
-            if un == NU - PERIOD + 1:
+        for st in range(EXP_OFF, NP + MX_OFF):
+            if 0 <= st - 1 < NP and on_vector(st - 1, 1, 1):
+                x_copy(st - 1, 1, 1)
+            if 0 <= st < NP:
+                for i in range(2):
+                    for a in range(2):
+                        x_transposes(st, i, a)
+                if st < MX_OFF:
+                    for i in range(EARLY):
+                        idle_pass(zc[:, 0:P], zs[:, 0:P], False)
+                for i in range(2):
+                    for a in range(2):
+                        if not on_vector(st, i, a):
+                            x_copy(st, i, a)
+            e_work(st, EXP_OFF, e_exp)
+            if st == 0:
+                for g in range(-ET_OFF):
+                    e_transposes(g)
+            e_work(st, EC_OFF, e_copy)
+            if 0 <= st - Q_OFF < NP:
+                x_quant(st - Q_OFF)
+            e_work(st, EQ_OFF, e_quant)
+            if st >= 0:
+                e_work(st, ET_OFF, e_transposes)
+            if 0 <= st - MX_OFF < NP:
+                for i in range(2):
+                    mx_pass(st - MX_OFF, i)
+            if 0 <= st < NP:
+                for i in range(2):
+                    tau, q = units[2 * st + i][0], units[2 * st + i][1]
+                    if q == tiles[tau][2] - 1:
+                        load_more(tau)
+            if st == NP:
                 nc.vector.tensor_reduce(out=rtot[:], in_=rs[:], axis=AX.X, op=ALU.add)
                 nc.vector.reciprocal(out=rinv[:], in_=rtot[:])
 

@@ -31,8 +31,8 @@ Q_OFF = 1
 MX_OFF = 3
 XGB = 3
 XCB = 4
-EARLY = 3
-WARM = ((3, 4), (4, 4), (5, 4))
+EARLY = 0
+WARM = ()
 VSKIP = 0
 
 
@@ -73,11 +73,6 @@ def tile_spatialgather_module_kernel(tc, feats, probs, out):
         ctx_sb = const.tile([P, C], F32, name="ctx_sb")
         o_sb = const.tile([P, C], F32, name="o_sb")
         acc = accp.tile([P, C], F32, name="acc")
-        zc = const.tile([P, C], U32, name="zc", align_bytes=64)
-        zs = const.tile([P, C], U8, name="zs", align_bytes=64)
-        zb = const.tile([P, 4 * C], BF16, name="zb", align_bytes=64)
-        gate_c = const.tile([P, len(WARM) * P], U32, name="gate_c", align_bytes=64)
-        gate_s = const.tile([P, len(WARM) * P], U8, name="gate_s", align_bytes=64)
 
         xs_tiles = {}
         xt_tiles = {}
@@ -153,19 +148,8 @@ def tile_spatialgather_module_kernel(tc, feats, probs, out):
                 lhsT_scale=e_sc[:, w0 : w0 + P],
                 rhs=xc[:, i * C : (i + 1) * C].bitcast(FP8X4),
                 rhs_scale=xsc[:, i * C : (i + 1) * C],
-                start=False,
+                start=(len(WARM) == 0 and st == 0 and i == 0),
                 stop=(st == NP - 1 and i == 1),
-            )
-
-        def idle_pass(codes, scale, first):
-            nc.tensor.matmul_mx(
-                out=acc[:],
-                lhsT=codes.bitcast(FP8X4),
-                lhsT_scale=scale,
-                rhs=zc[:].bitcast(FP8X4),
-                rhs_scale=zs[:],
-                start=first,
-                stop=False,
             )
 
         def e_exp(g):
@@ -226,8 +210,6 @@ def tile_spatialgather_module_kernel(tc, feats, probs, out):
         nc.vector.memset(scr0[:], 0.0)
         nc.vector.memset(e_codes[:].bitcast(I32), 0)
         nc.vector.memset(e_sc[:].bitcast(I32), 0)
-        nc.vector.memset(zb[:].bitcast(I32), 0)
-        nc.vector.quantize_mx(out=zc[:].bitcast(FP8X4), scales=zs[:], in_=zb[:])
         nc.scalar.activation(out=scr1[:], in_=scr0[:], func=ACT.Exp)
 
         off = 0
@@ -243,12 +225,6 @@ def tile_spatialgather_module_kernel(tc, feats, probs, out):
                 accum_out=mcol[:, i : i + 1],
             )
             off += w
-            for k, (chunk, count) in enumerate(WARM):
-                if chunk == i:
-                    cols = slice(k * P, (k + 1) * P)
-                    nc.vector.quantize_mx(out=gate_c[:, cols].bitcast(FP8X4), scales=gate_s[:, cols], in_=zb[:, 0:C])
-                    for j in range(count):
-                        idle_pass(gate_c[:, cols], gate_s[:, cols], k == 0 and j == 0)
         nc.vector.tensor_reduce(out=mall[:], in_=mcol[:, 0 : len(PROB_CHUNKS)], axis=AX.X, op=ALU.max)
         nc.vector.tensor_scalar(out=negmax[:], in0=mall[:], scalar1=-1.0, scalar2=None, op0=ALU.mult)
 
@@ -263,9 +239,6 @@ def tile_spatialgather_module_kernel(tc, feats, probs, out):
                 for i in range(2):
                     for a in range(2):
                         x_transposes(st, i, a)
-                if st < MX_OFF:
-                    for i in range(EARLY):
-                        idle_pass(zc[:, 0:P], zs[:, 0:P], False)
                 for i in range(2):
                     for a in range(2):
                         if not on_vector(st, i, a):

@@ -33,7 +33,7 @@ XGB = 3
 XCB = 4
 EARLY = 0
 WARM = ()
-VSKIP = 0
+VSKIP = 8
 
 
 def tile_spatialgather_module_kernel(tc, feats, probs, out):

from contextlib import ExitStack

import concourse.mybir as mybir
from concourse.masks import make_identity

F32 = mybir.dt.float32
BF16 = mybir.dt.bfloat16
U32 = mybir.dt.uint32
U8 = mybir.dt.uint8
I32 = mybir.dt.int32
FP8X4 = mybir.dt.float8_e4m3fn_x4
ALU = mybir.AluOpType
ACT = mybir.ActivationFunctionType
AX = mybir.AxisListType

P = 128
B, C, K, N = 2, 512, 64, 16384
FLOPS = 2 * B * K * C * N

NP = N // 512
PROB_CHUNKS = (2048, 2048, 2048, 2048, 2048, 2048, 2048, 1024, 1024)
CHUNKS = (1, 1, 2, 4, 4, 4, 4, 4, 4, 2, 1, 1)
XBUFS = {1: 4, 2: 2, 4: 5}
ESTEP = 192
ER = 8
EXP_OFF = -2
ET_OFF = -1
EC_OFF = 0
EQ_OFF = 0
Q_OFF = 1
MX_OFF = 3
XGB = 3
XCB = 4
EARLY = 0
WARM = ()
VSKIP = 8


def tile_spatialgather_module_kernel(tc, feats, probs, out):
    nc = tc.nc
    x = feats.rearrange("b c h w -> b c (h w)")
    l = probs.rearrange("b k h w -> (b k) (h w)")
    o = out.rearrange("b (t p) k o -> p (b t) (k o)", p=P)

    with ExitStack() as ctx:
        const = ctx.enter_context(tc.tile_pool(name="const", bufs=1))
        xsp = ctx.enter_context(tc.tile_pool(name="xsp", bufs=1))
        xgp = ctx.enter_context(tc.tile_pool(name="xgp", bufs=XGB))
        xcp = ctx.enter_context(tc.tile_pool(name="xcp", bufs=XCB))
        jkp = ctx.enter_context(tc.tile_pool(name="jkp", bufs=2))
        enp = ctx.enter_context(tc.tile_pool(name="enp", bufs=4))
        egp = ctx.enter_context(tc.tile_pool(name="egp", bufs=3))
        accp = ctx.enter_context(tc.psum_pool(name="accp", bufs=1))
        tps = ctx.enter_context(tc.psum_pool(name="tps", bufs=4))
        tpv = ctx.enter_context(tc.psum_pool(name="tpv", bufs=2))
        tpe = ctx.enter_context(tc.psum_pool(name="tpe", bufs=1))
        ctx.enter_context(tc.manual_schedule())

        ident_f = const.tile([P, P], F32, name="ident_f")
        ident_b = const.tile([P, P], BF16, name="ident_b")
        perm_b = const.tile([P, P], BF16, name="perm_b")
        l_sb = const.tile([P, N], BF16, name="l_sb")
        e_codes = const.tile([P, ER * ESTEP + 64], U32, name="e_codes", align_bytes=64)
        e_sc = const.tile([P, ER * ESTEP + 64], U8, name="e_sc", align_bytes=64)
        mcol = const.tile([P, 16], F32, name="mcol")
        mall = const.tile([P, 1], F32, name="mall")
        negmax = const.tile([P, 1], F32, name="negmax")
        rs = const.tile([P, NP], F32, name="rs")
        rtot = const.tile([P, 1], F32, name="rtot")
        rinv = const.tile([P, 1], F32, name="rinv")
        scr0 = const.tile([P, 1], F32, name="scr0")
        scr1 = const.tile([P, 1], F32, name="scr1")
        ctx_sb = const.tile([P, C], F32, name="ctx_sb")
        o_sb = const.tile([P, C], F32, name="o_sb")
        acc = accp.tile([P, C], F32, name="acc")

        xs_tiles = {}
        xt_tiles = {}
        xg_tiles = {}
        xc_tiles = {}
        en_tiles = {}
        et_tiles = {}
        eg_tiles = {}

        tiles = []
        units = []
        g0 = 0
        for ng in CHUNKS:
            for b in range(B):
                for q in range(ng):
                    units.append((len(tiles), q, b, g0 + q))
                tiles.append((b, g0, ng))
            g0 += ng

        def load_x(tau):
            b, g0, ng = tiles[tau]
            xs = xsp.tile([P, 4 * 512 * ng], BF16, name="xs%d" % ng, tag="xs%d" % ng, bufs=XBUFS[ng])
            nc.sync.dma_start(
                out=xs[:].rearrange("p (c n) -> p c n", c=4),
                in_=x[b, :, g0 * 512 : (g0 + ng) * 512].rearrange("(c p) n -> p c n", p=P),
            )
            xs_tiles[tau] = xs

        def on_vector(st, i, a):
            return i == 1 and a == 1 and not (VSKIP and st % VSKIP == VSKIP - 1)

        def x_transposes(st, i, a):
            tau, q = units[2 * st + i][0], units[2 * st + i][1]
            row = 256 * tiles[tau][2]
            xw = xs_tiles[tau][:].bitcast(F32)
            if on_vector(st, i, a):
                xt = tpv.tile([P, 4, P], F32, name="xtv", tag="xtv")
            else:
                xt = tps.tile([P, 4, P], F32, name="xts", tag="xts")
            for aa in range(2):
                for u in range(2):
                    w0 = (2 * a + aa) * row + q * 256 + u * P
                    nc.tensor.transpose(xt[:, 2 * aa + u, :], xw[:, w0 : w0 + P], ident_f[:])
            xt_tiles[(st, i, a)] = xt

        def x_copy(st, i, a):
            xt = xt_tiles[(st, i, a)]
            if i == 0 and a == 0:
                xg = xgp.tile([P, 4096], BF16, name="xg", tag="xg", align_bytes=64)
                xg_tiles[st] = xg
            xg = xg_tiles[st]
            h0 = (2 * i + a) * 1024
            dst = xg[:, h0 : h0 + 1024].bitcast(F32).rearrange("p (a c u) -> p a c u", a=2, u=2)
            src = xt[:].rearrange("p (a u) c -> p a c u", u=2)
            if on_vector(st, i, a):
                nc.vector.tensor_copy(out=dst, in_=src)
            else:
                nc.scalar.copy(out=dst, in_=src)

        def x_quant(st):
            xc = xcp.tile([P, 2 * C], U32, name="xc", tag="xc", align_bytes=64)
            xsc = xcp.tile([P, 2 * C], U8, name="xsc", tag="xsc", align_bytes=64)
            xc_tiles[st] = (xc, xsc)
            nc.vector.quantize_mx(out=xc[:].bitcast(FP8X4), scales=xsc[:], in_=xg_tiles[st][:])

        def mx_pass(st, i):
            b, g = units[2 * st + i][2], units[2 * st + i][3]
            xc, xsc = xc_tiles[st]
            w0 = (g % ER) * ESTEP + (1 - b) * P
            nc.tensor.matmul_mx(
                out=acc[:],
                lhsT=e_codes[:, w0 : w0 + P].bitcast(FP8X4),
                lhsT_scale=e_sc[:, w0 : w0 + P],
                rhs=xc[:, i * C : (i + 1) * C].bitcast(FP8X4),
                rhs_scale=xsc[:, i * C : (i + 1) * C],
                start=(len(WARM) == 0 and st == 0 and i == 0),
                stop=(st == NP - 1 and i == 1),
            )

        def e_exp(g):
            en = enp.tile([P, 512], BF16, name="en", tag="en")
            nc.scalar.activation(
                out=en[:],
                in_=l_sb[:, g * 512 : (g + 1) * 512],
                func=ACT.Exp,
                bias=negmax[:, 0:1],
                scale=1.0,
                accum_out=rs[:, g : g + 1],
            )
            en_tiles[g] = en

        def e_transposes(g):
            v = en_tiles[g][:].rearrange("p (u q e) -> p u e q", u=2, e=2)
            et = tpe.tile([P, 4, P], BF16, name="et", tag="et")
            for u in range(2):
                for e in range(2):
                    nc.tensor.transpose(et[:, 2 * u + e, :], v[:, u, e, :], perm_b[:])
            et_tiles[g] = et

        def e_copy(g):
            eg = egp.tile([P, 512], BF16, name="eg", tag="eg", align_bytes=64)
            nc.vector.tensor_copy(
                out=eg[:].rearrange("p (r t) -> p r t", t=4), in_=et_tiles[g][:].rearrange("p t r -> p r t")
            )
            eg_tiles[g] = eg

        def e_quant(g):
            w0 = (g % ER) * ESTEP + 64
            nc.vector.quantize_mx(
                out=e_codes[:, w0 : w0 + P].bitcast(FP8X4), scales=e_sc[:, w0 : w0 + P], in_=eg_tiles[g][:]
            )

        off = 0
        for w in PROB_CHUNKS:
            nc.sync.dma_start(out=l_sb[:, off : off + w], in_=l[:, off : off + w])
            off += w
        holder = []
        for tau in range(len(tiles)):
            same = [t for t in range(tau) if tiles[t][2] == tiles[tau][2]]
            nb = XBUFS[tiles[tau][2]]
            holder.append(same[-nb] if len(same) >= nb else -1)
        loaded = [0]

        def load_more(done):
            while loaded[0] < len(tiles) and holder[loaded[0]] <= done:
                load_x(loaded[0])
                loaded[0] += 1

        load_more(-1)

        make_identity(nc, ident_f[:])
        make_identity(nc, ident_b[:])
        nc.gpsimd.tensor_copy(out=perm_b[:, 0:64], in_=ident_b[:, 64:128])
        nc.gpsimd.tensor_copy(out=perm_b[:, 64:128], in_=ident_b[:, 0:64])
        nc.vector.memset(scr0[:], 0.0)
        nc.vector.memset(e_codes[:].bitcast(I32), 0)
        nc.vector.memset(e_sc[:].bitcast(I32), 0)
        nc.scalar.activation(out=scr1[:], in_=scr0[:], func=ACT.Exp)

        off = 0
        for i, w in enumerate(PROB_CHUNKS):
            junk = jkp.tile([P, w], BF16, name="junk", tag="junk")
            nc.vector.tensor_scalar(
                out=junk[:],
                in0=l_sb[:, off : off + w],
                scalar1=0.0,
                scalar2=None,
                op0=ALU.add,
                op1=ALU.max,
                accum_out=mcol[:, i : i + 1],
            )
            off += w
        nc.vector.tensor_reduce(out=mall[:], in_=mcol[:, 0 : len(PROB_CHUNKS)], axis=AX.X, op=ALU.max)
        nc.vector.tensor_scalar(out=negmax[:], in0=mall[:], scalar1=-1.0, scalar2=None, op0=ALU.mult)

        def e_work(st, off, fn):
            if 0 <= st - off < NP:
                fn(st - off)

        for st in range(EXP_OFF, NP + MX_OFF):
            if 0 <= st - 1 < NP and on_vector(st - 1, 1, 1):
                x_copy(st - 1, 1, 1)
            if 0 <= st < NP:
                for i in range(2):
                    for a in range(2):
                        x_transposes(st, i, a)
                for i in range(2):
                    for a in range(2):
                        if not on_vector(st, i, a):
                            x_copy(st, i, a)
            e_work(st, EXP_OFF, e_exp)
            if st == 0:
                for g in range(-ET_OFF):
                    e_transposes(g)
            e_work(st, EC_OFF, e_copy)
            if 0 <= st - Q_OFF < NP:
                x_quant(st - Q_OFF)
            e_work(st, EQ_OFF, e_quant)
            if st >= 0:
                e_work(st, ET_OFF, e_transposes)
            if 0 <= st - MX_OFF < NP:
                for i in range(2):
                    mx_pass(st - MX_OFF, i)
            if 0 <= st < NP:
                for i in range(2):
                    tau, q = units[2 * st + i][0], units[2 * st + i][1]
                    if q == tiles[tau][2] - 1:
                        load_more(tau)
            if st == NP:
                nc.vector.tensor_reduce(out=rtot[:], in_=rs[:], axis=AX.X, op=ALU.add)
                nc.vector.reciprocal(out=rinv[:], in_=rtot[:])

        o_v = o_sb[:].rearrange("p (b t k) -> p b t k", b=B, k=K)
        for a in range(2):
            nc.vector.tensor_scalar(
                out=ctx_sb[:, a * 256 : (a + 1) * 256],
                in0=acc[:, a * 256 : (a + 1) * 256],
                scalar1=rinv[:, 0:1],
                scalar2=None,
                op0=ALU.mult,
            )
            if a == 0:
                ot = tpv.tile([P, 2, P], F32, name="otv", tag="xtv")
            else:
                ot = tps.tile([P, 2, P], F32, name="ots", tag="xts")
            for i in range(2):
                t = 2 * a + i
                nc.tensor.transpose(ot[:, i, :], ctx_sb[:, t * P : (t + 1) * P], ident_f[:])
            src = ot[:].rearrange("p t (b k) -> p b t k", b=B)
            if a == 0:
                nc.scalar.copy(out=o_v[:, :, 0:2, :], in_=src)
            else:
                nc.vector.tensor_copy(out=o_v[:, :, 2:4, :], in_=src)
        nc.sync.dma_start(out=o, in_=o_sb[:].rearrange("p (g k) -> p g k", k=K))
